import numpy as np
import ml_dtypes

BF16 = ml_dtypes.bfloat16


def bf(x):
    return np.asarray(x, np.float32).astype(BF16)


def f32(x):
    return np.asarray(x, np.float32)


def f64(x):
    return np.asarray(x).astype(np.float64)


def striped(idx):
    return np.tile(idx.reshape(-1, 16).T, (8, 1))


V, D, E, R, OD, N = 2048, 128, 8, 16, 256, 512
M = E * R
SCALING = 2.0


def setup_inputs():
    table = bf(np.random.standard_normal((V, D)))
    a = bf(np.random.standard_normal((D, M)) / np.sqrt(D))
    w_route = bf(np.repeat(np.random.standard_normal((D, E)) / np.sqrt(D), R, axis=1))
    bw = bf(np.random.standard_normal((M, OD)) / np.sqrt(R))
    return {"table": table, "a": a, "w_route": w_route, "bw": bw, "offs": striped(np.random.permutation(V)[:N])}


def reference(table, a, w_route, bw, offs):
    idx = offs[:16].T.reshape(-1)
    xt = f64(table)[idx].T
    h = f64(a).T @ xt
    p = np.exp(f64(w_route).T @ xt)
    route = R * p / p.sum(axis=0, keepdims=True)
    return SCALING * (f64(bw).T @ (h * route))

@@ -1,0 +1,104 @@
+import concourse.masks as masks
+import concourse.mybir as mybir
+
+BF16, F32, U16 = mybir.dt.bfloat16, mybir.dt.float32, mybir.dt.uint16
+ACT = mybir.ActivationFunctionType
+ALU = mybir.AluOpType
+
+V, D, E, R, OD, N = 2048, 128, 8, 16, 256, 512
+M = E * R
+P = 128
+SCALING = 2.0
+FLOPS = 2 * N * (D * M + D * M + M * OD)
+
+GROUP = 4
+GROUPS = V // P // GROUP
+
+EXP_CAP = 1.0e30
+
+
+def tile_moelora_kernel(tc, table, a, w_route, bw, offs, out):
+    nc = tc.nc
+    with (
+        tc.tile_pool(name="held", bufs=1) as held,
+        tc.psum_pool(name="psum", bufs=1) as psum,
+        tc.psum_pool(name="turned", bufs=2) as turned,
+    ):
+        offsets = held.tile([P, N // 16], U16, name="offsets")
+        nc.sync.dma_start(offsets[:], offs)
+
+        w_sb = held.tile([D, M], BF16, name="w_sb")
+        nc.scalar.dma_start(w_sb[:], w_route)
+
+        table_sb = held.tile([P, V // P, D], BF16, name="table_sb")
+        table_blocks = table.rearrange("(b p) d -> p b d", p=P)
+        for g in range(GROUPS):
+            queue = nc.sync if g % 2 == 0 else nc.scalar
+            blocks = slice(g * GROUP, (g + 1) * GROUP)
+            queue.dma_start(table_sb[:, blocks, :], table_blocks[:, blocks, :])
+
+        a_sb = held.tile([D, M], BF16, name="a_sb")
+        nc.sync.dma_start(a_sb[:], a)
+        bw_sb = held.tile([M, OD], BF16, name="bw_sb")
+        nc.scalar.dma_start(bw_sb[:], bw)
+
+        identity = held.tile([P, P], BF16, name="identity")
+        masks.make_identity(nc, identity[:])
+
+        in_expert = held.tile([M, E], F32, name="in_expert")
+        nc.vector.reduce_sum(in_expert[:], identity[:].rearrange("k (e r) -> k e r", r=R), axis=mybir.AxisListType.X)
+        same_expert = held.tile([M, M], BF16, name="same_expert")
+        nc.vector.tensor_scalar_mul(
+            same_expert[:].rearrange("k (e r) -> k e r", r=R),
+            in_expert[:].unsqueeze(2).to_broadcast([M, E, R]),
+            1.0 / (2.0 * SCALING),
+        )
+
+        w_diff = held.tile([D, M], BF16, name="w_diff")
+        w_of_f = w_sb[:].rearrange("d (f r) -> d f r", r=R)[:, :, 0]
+        nc.vector.tensor_tensor(
+            w_diff[:].rearrange("d (g f) -> d g f", f=E),
+            w_of_f.unsqueeze(1).to_broadcast([D, M // E, E]),
+            w_sb[:].rearrange("d (g f) -> d g f", f=E),
+            ALU.subtract,
+        )
+
+        table_t = held.tile([D, V], BF16, name="table_t")
+        for g in range(GROUPS):
+            turned_ps = turned.tile([D, GROUP * P], BF16, name="turned_ps")
+            for k in range(GROUP):
+                nc.tensor.transpose(turned_ps[:, k * P : (k + 1) * P], table_sb[:, g * GROUP + k, :], identity[:])
+            columns = slice(g * GROUP * P, (g + 1) * GROUP * P)
+            if g % 2 == 0:
+                nc.vector.tensor_copy(table_t[:, columns], turned_ps[:])
+            else:
+                nc.scalar.copy(table_t[:, columns], turned_ps[:])
+
+        diff_ps = psum.tile([M, N], F32, name="diff_ps")
+        nc.tensor.matmul(diff_ps[:], w_diff[:], table_t[:].indirect(offsets[:]), start=True, stop=True)
+        h_ps = psum.tile([M, N], F32, name="h_ps")
+        nc.tensor.matmul(h_ps[:], a_sb[:], table_t[:].indirect(offsets[:]), start=True, stop=True)
+
+        expd = held.tile([M, N], BF16, name="expd")
+        nc.scalar.activation(expd[:], diff_ps[:], ACT.Exp)
+        nc.vector.tensor_scalar_min(expd[:], expd[:], EXP_CAP)
+
+        denom_ps = psum.tile([M, N], F32, name="denom_ps")
+        nc.tensor.matmul(denom_ps[:], same_expert[:], expd[:], start=True, stop=True)
+
+        route = held.tile([M, N], F32, name="route")
+        nc.vector.reciprocal(route[:], denom_ps[:])
+
+        wh = held.tile([M, N], BF16, name="wh")
+        nc.vector.tensor_tensor(wh[:], h_ps[:], route[:], ALU.mult)
+
+        for ob in range(OD // P):
+            out_ps = psum.tile([P, N], F32, name=f"out_ps{ob}")
+            nc.tensor.matmul(out_ps[:], bw_sb[:, ob * P : (ob + 1) * P], wh[:], start=True, stop=True)
+            out_sb = held.tile([P, N], F32, name=f"out_sb{ob}")
+            if ob == 0:
+                nc.vector.tensor_copy(out_sb[:], out_ps[:])
+                nc.sync.dma_start(out[ob * P : (ob + 1) * P, :], out_sb[:])
+            else:
+                nc.scalar.copy(out_sb[:], out_ps[:])
+                nc.scalar.dma_start(out[ob * P : (ob + 1) * P, :], out_sb[:])

@@ -14,6 +14,8 @@ FLOPS = 2 * N * (D * M + D * M + M * OD)
 GROUP = 4
 GROUPS = V // P // GROUP
 
+WARM_MATMULS = 6
+
 EXP_CAP = 1.0e30
 
 
@@ -41,6 +43,12 @@ def tile_moelora_kernel(tc, table, a, w_route, bw, offs, out):
         nc.sync.dma_start(a_sb[:], a)
         bw_sb = held.tile([M, OD], BF16, name="bw_sb")
         nc.scalar.dma_start(bw_sb[:], bw)
+
+        zeros = held.tile([P, N], BF16, name="zeros")
+        nc.vector.memset(zeros[:], 0.0)
+        unused_ps = psum.tile([P, N], F32, name="unused_ps")
+        for i in range(WARM_MATMULS):
+            nc.tensor.matmul(unused_ps[:], zeros[:, 0:P], zeros[:], start=True, stop=True)
 
         identity = held.tile([P, P], BF16, name="identity")
         masks.make_identity(nc, identity[:])

@@ -13,8 +13,9 @@ FLOPS = 2 * N * (D * M + D * M + M * OD)
 
 GROUP = 4
 GROUPS = V // P // GROUP
-
-WARM_MATMULS = 6
+PIECES = 2
+PIECE = N // PIECES
+BLOCKS = PIECE // P
 
 EXP_CAP = 1.0e30
 
@@ -23,8 +24,8 @@ def tile_moelora_kernel(tc, table, a, w_route, bw, offs, out):
     nc = tc.nc
     with (
         tc.tile_pool(name="held", bufs=1) as held,
-        tc.psum_pool(name="psum", bufs=1) as psum,
-        tc.psum_pool(name="turned", bufs=2) as turned,
+        tc.psum_pool(name="single", bufs=1) as single,
+        tc.psum_pool(name="double", bufs=2) as double,
     ):
         offsets = held.tile([P, N // 16], U16, name="offsets")
         nc.sync.dma_start(offsets[:], offs)
@@ -44,36 +45,28 @@ def tile_moelora_kernel(tc, table, a, w_route, bw, offs, out):
         bw_sb = held.tile([M, OD], BF16, name="bw_sb")
         nc.scalar.dma_start(bw_sb[:], bw)
 
-        zeros = held.tile([P, N], BF16, name="zeros")
-        nc.vector.memset(zeros[:], 0.0)
-        unused_ps = psum.tile([P, N], F32, name="unused_ps")
-        for i in range(WARM_MATMULS):
-            nc.tensor.matmul(unused_ps[:], zeros[:, 0:P], zeros[:], start=True, stop=True)
-
         identity = held.tile([P, P], BF16, name="identity")
         masks.make_identity(nc, identity[:])
+        identity_f32 = held.tile([P, P], F32, name="identity_f32")
+        nc.vector.tensor_copy(identity_f32[:], identity[:])
 
         in_expert = held.tile([M, E], F32, name="in_expert")
         nc.vector.reduce_sum(in_expert[:], identity[:].rearrange("k (e r) -> k e r", r=R), axis=mybir.AxisListType.X)
-        same_expert = held.tile([M, M], BF16, name="same_expert")
-        nc.vector.tensor_scalar_mul(
-            same_expert[:].rearrange("k (e r) -> k e r", r=R),
-            in_expert[:].unsqueeze(2).to_broadcast([M, E, R]),
-            1.0 / (2.0 * SCALING),
-        )
+        adder = held.tile([M, E], BF16, name="adder")
+        nc.vector.tensor_scalar_mul(adder[:], in_expert[:], 1.0 / (2.0 * SCALING))
 
         w_diff = held.tile([D, M], BF16, name="w_diff")
         w_of_f = w_sb[:].rearrange("d (f r) -> d f r", r=R)[:, :, 0]
         nc.vector.tensor_tensor(
-            w_diff[:].rearrange("d (g f) -> d g f", f=E),
+            w_diff[:].rearrange("d (c f) -> d c f", f=E),
             w_of_f.unsqueeze(1).to_broadcast([D, M // E, E]),
-            w_sb[:].rearrange("d (g f) -> d g f", f=E),
+            w_sb[:].rearrange("d (c f) -> d c f", f=E),
             ALU.subtract,
         )
 
         table_t = held.tile([D, V], BF16, name="table_t")
         for g in range(GROUPS):
-            turned_ps = turned.tile([D, GROUP * P], BF16, name="turned_ps")
+            turned_ps = double.tile([D, GROUP * P], BF16, name="turned_ps", tag="turned_or_out")
             for k in range(GROUP):
                 nc.tensor.transpose(turned_ps[:, k * P : (k + 1) * P], table_sb[:, g * GROUP + k, :], identity[:])
             columns = slice(g * GROUP * P, (g + 1) * GROUP * P)
@@ -82,31 +75,56 @@ def tile_moelora_kernel(tc, table, a, w_route, bw, offs, out):
             else:
                 nc.scalar.copy(table_t[:, columns], turned_ps[:])
 
-        diff_ps = psum.tile([M, N], F32, name="diff_ps")
-        nc.tensor.matmul(diff_ps[:], w_diff[:], table_t[:].indirect(offsets[:]), start=True, stop=True)
-        h_ps = psum.tile([M, N], F32, name="h_ps")
-        nc.tensor.matmul(h_ps[:], a_sb[:], table_t[:].indirect(offsets[:]), start=True, stop=True)
+        list_piece = [offsets[:, i * (PIECE // 16) : (i + 1) * (PIECE // 16)] for i in range(PIECES)]
+        tokens = [slice(i * PIECE, (i + 1) * PIECE) for i in range(PIECES)]
+
+        diff_ps = [double.tile([M, PIECE], F32, name=f"diff_ps{i}", tag="diff_ps") for i in range(PIECES)]
+        for i in range(PIECES):
+            nc.tensor.matmul(diff_ps[i][:], w_diff[:], table_t[:].indirect(list_piece[i]), start=True, stop=True)
+        h_ps = single.tile([M, N], F32, name="h_ps")
+        for i in range(PIECES):
+            nc.tensor.matmul(h_ps[:, tokens[i]], a_sb[:], table_t[:].indirect(list_piece[i]), start=True, stop=True)
 
         expd = held.tile([M, N], BF16, name="expd")
-        nc.scalar.activation(expd[:], diff_ps[:], ACT.Exp)
-        nc.vector.tensor_scalar_min(expd[:], expd[:], EXP_CAP)
+        for i in range(PIECES):
+            nc.scalar.activation(expd[:, tokens[i]], diff_ps[i][:], ACT.Exp)
+            nc.vector.tensor_scalar_min(expd[:, tokens[i]], expd[:, tokens[i]], EXP_CAP)
 
-        denom_ps = psum.tile([M, N], F32, name="denom_ps")
-        nc.tensor.matmul(denom_ps[:], same_expert[:], expd[:], start=True, stop=True)
+        h_sb = held.tile([M, N], F32, name="h_sb")
+        nc.scalar.copy(h_sb[:], h_ps[:])
 
-        route = held.tile([M, N], F32, name="route")
-        nc.vector.reciprocal(route[:], denom_ps[:])
+        denom_t_ps = single.tile([P, (N // P) * E], F32, name="denom_t_ps")
+        route_t = held.tile([P, (N // P) * E], F32, name="route_t")
+        route_t_rows = held.tile([P, N], F32, name="route_t_rows")
+        for i in range(PIECES):
+            for b in range(i * BLOCKS, (i + 1) * BLOCKS):
+                nc.tensor.matmul(
+                    denom_t_ps[:, b * E : (b + 1) * E], expd[:, b * P : (b + 1) * P], adder[:], start=True, stop=True
+                )
+            experts = slice(i * BLOCKS * E, (i + 1) * BLOCKS * E)
+            nc.vector.reciprocal(route_t[:, experts], denom_t_ps[:, experts])
+            nc.vector.tensor_copy(
+                route_t_rows[:, tokens[i]].rearrange("t (c r) -> t c r", r=R),
+                route_t[:, experts].unsqueeze(2).to_broadcast([P, BLOCKS * E, R]),
+            )
 
         wh = held.tile([M, N], BF16, name="wh")
-        nc.vector.tensor_tensor(wh[:], h_ps[:], route[:], ALU.mult)
+        for i in range(PIECES):
+            route_ps = double.tile([M, PIECE], F32, name="route_ps")
+            for k in range(BLOCKS):
+                b = i * BLOCKS + k
+                nc.tensor.transpose(route_ps[:, k * P : (k + 1) * P], route_t_rows[:, b * P : (b + 1) * P], identity_f32[:])
+            nc.vector.tensor_tensor(wh[:, tokens[i]], route_ps[:], h_sb[:, tokens[i]], ALU.mult)
 
-        for ob in range(OD // P):
-            out_ps = psum.tile([P, N], F32, name=f"out_ps{ob}")
-            nc.tensor.matmul(out_ps[:], bw_sb[:, ob * P : (ob + 1) * P], wh[:], start=True, stop=True)
-            out_sb = held.tile([P, N], F32, name=f"out_sb{ob}")
-            if ob == 0:
-                nc.vector.tensor_copy(out_sb[:], out_ps[:])
-                nc.sync.dma_start(out[ob * P : (ob + 1) * P, :], out_sb[:])
-            else:
-                nc.scalar.copy(out_sb[:], out_ps[:])
-                nc.scalar.dma_start(out[ob * P : (ob + 1) * P, :], out_sb[:])
+        for i in range(PIECES):
+            for ob in range(OD // P):
+                features = slice(ob * P, (ob + 1) * P)
+                out_ps = double.tile([P, PIECE], F32, name="out_ps", tag="turned_or_out")
+                nc.tensor.matmul(out_ps[:], bw_sb[:, features], wh[:, tokens[i]], start=True, stop=True)
+                out_sb = held.tile([P, PIECE], F32, name=f"out_sb{i}{ob}")
+                if ob == 0:
+                    nc.vector.tensor_copy(out_sb[:], out_ps[:])
+                    nc.sync.dma_start(out[features, tokens[i]], out_sb[:])
+                else:
+                    nc.scalar.copy(out_sb[:], out_ps[:])
+                    nc.scalar.dma_start(out[features, tokens[i]], out_sb[:])

@@ -11,7 +11,9 @@ P = 128
 SCALING = 2.0
 FLOPS = 2 * N * (D * M + D * M + M * OD)
 
-GROUP = 4
+LOAD = 4
+LOADS = V // P // LOAD
+GROUP = 2
 GROUPS = V // P // GROUP
 PIECES = 2
 PIECE = N // PIECES
@@ -25,24 +27,22 @@ def tile_moelora_kernel(tc, table, a, w_route, bw, offs, out):
     with (
         tc.tile_pool(name="held", bufs=1) as held,
         tc.psum_pool(name="single", bufs=1) as single,
-        tc.psum_pool(name="double", bufs=2) as double,
+        tc.psum_pool(name="work", bufs=6) as work,
     ):
-        offsets = held.tile([P, N // 16], U16, name="offsets")
-        nc.sync.dma_start(offsets[:], offs)
-
-        w_sb = held.tile([D, M], BF16, name="w_sb")
-        nc.scalar.dma_start(w_sb[:], w_route)
-
         table_sb = held.tile([P, V // P, D], BF16, name="table_sb")
         table_blocks = table.rearrange("(b p) d -> p b d", p=P)
-        for g in range(GROUPS):
-            queue = nc.sync if g % 2 == 0 else nc.scalar
-            blocks = slice(g * GROUP, (g + 1) * GROUP)
-            queue.dma_start(table_sb[:, blocks, :], table_blocks[:, blocks, :])
-
+        w_sb = held.tile([D, M], BF16, name="w_sb")
+        offsets = held.tile([P, N // 16], U16, name="offsets")
         a_sb = held.tile([D, M], BF16, name="a_sb")
-        nc.sync.dma_start(a_sb[:], a)
         bw_sb = held.tile([M, OD], BF16, name="bw_sb")
+
+        nc.scalar.dma_start(w_sb[:], w_route)
+        for q in range(LOADS):
+            queue = nc.sync if q < LOADS - 1 else nc.scalar
+            blocks = slice(q * LOAD, (q + 1) * LOAD)
+            queue.dma_start(table_sb[:, blocks, :], table_blocks[:, blocks, :])
+        nc.sync.dma_start(offsets[:], offs)
+        nc.scalar.dma_start(a_sb[:], a)
         nc.scalar.dma_start(bw_sb[:], bw)
 
         identity = held.tile([P, P], BF16, name="identity")
@@ -66,19 +66,19 @@ def tile_moelora_kernel(tc, table, a, w_route, bw, offs, out):
 
         table_t = held.tile([D, V], BF16, name="table_t")
         for g in range(GROUPS):
-            turned_ps = double.tile([D, GROUP * P], BF16, name="turned_ps", tag="turned_or_out")
+            turned_ps = work.tile([D, GROUP * P], BF16, name="turned_ps", tag="work")
             for k in range(GROUP):
                 nc.tensor.transpose(turned_ps[:, k * P : (k + 1) * P], table_sb[:, g * GROUP + k, :], identity[:])
             columns = slice(g * GROUP * P, (g + 1) * GROUP * P)
             if g % 2 == 0:
-                nc.vector.tensor_copy(table_t[:, columns], turned_ps[:])
-            else:
                 nc.scalar.copy(table_t[:, columns], turned_ps[:])
+            else:
+                nc.vector.tensor_copy(table_t[:, columns], turned_ps[:])
 
         list_piece = [offsets[:, i * (PIECE // 16) : (i + 1) * (PIECE // 16)] for i in range(PIECES)]
         tokens = [slice(i * PIECE, (i + 1) * PIECE) for i in range(PIECES)]
 
-        diff_ps = [double.tile([M, PIECE], F32, name=f"diff_ps{i}", tag="diff_ps") for i in range(PIECES)]
+        diff_ps = [work.tile([M, PIECE], F32, name=f"diff_ps{i}", tag="work") for i in range(PIECES)]
         for i in range(PIECES):
             nc.tensor.matmul(diff_ps[i][:], w_diff[:], table_t[:].indirect(list_piece[i]), start=True, stop=True)
         h_ps = single.tile([M, N], F32, name="h_ps")
@@ -110,7 +110,7 @@ def tile_moelora_kernel(tc, table, a, w_route, bw, offs, out):
 
         wh = held.tile([M, N], BF16, name="wh")
         for i in range(PIECES):
-            route_ps = double.tile([M, PIECE], F32, name="route_ps")
+            route_ps = work.tile([M, PIECE], F32, name="route_ps", tag="work")
             for k in range(BLOCKS):
                 b = i * BLOCKS + k
                 nc.tensor.transpose(route_ps[:, k * P : (k + 1) * P], route_t_rows[:, b * P : (b + 1) * P], identity_f32[:])
@@ -119,7 +119,7 @@ def tile_moelora_kernel(tc, table, a, w_route, bw, offs, out):
         for i in range(PIECES):
             for ob in range(OD // P):
                 features = slice(ob * P, (ob + 1) * P)
-                out_ps = double.tile([P, PIECE], F32, name="out_ps", tag="turned_or_out")
+                out_ps = work.tile([P, PIECE], F32, name="out_ps", tag="work")
                 nc.tensor.matmul(out_ps[:], bw_sb[:, features], wh[:, tokens[i]], start=True, stop=True)
                 out_sb = held.tile([P, PIECE], F32, name=f"out_sb{i}{ob}")
                 if ob == 0:

@@ -11,8 +11,7 @@ P = 128
 SCALING = 2.0
 FLOPS = 2 * N * (D * M + D * M + M * OD)
 
-LOAD = 4
-LOADS = V // P // LOAD
+LOAD_STARTS = (0, 2, 4, 8, 12, 16)
 GROUP = 2
 GROUPS = V // P // GROUP
 PIECES = 2
@@ -37,13 +36,13 @@ def tile_moelora_kernel(tc, table, a, w_route, bw, offs, out):
         bw_sb = held.tile([M, OD], BF16, name="bw_sb")
 
         nc.scalar.dma_start(w_sb[:], w_route)
-        for q in range(LOADS):
-            queue = nc.sync if q < LOADS - 1 else nc.scalar
-            blocks = slice(q * LOAD, (q + 1) * LOAD)
+        for q in range(len(LOAD_STARTS) - 1):
+            queue = nc.scalar if q in (2, 4) else nc.sync
+            blocks = slice(LOAD_STARTS[q], LOAD_STARTS[q + 1])
             queue.dma_start(table_sb[:, blocks, :], table_blocks[:, blocks, :])
         nc.sync.dma_start(offsets[:], offs)
         nc.scalar.dma_start(a_sb[:], a)
-        nc.scalar.dma_start(bw_sb[:], bw)
+        nc.sync.dma_start(bw_sb[:], bw)
 
         identity = held.tile([P, P], BF16, name="identity")
         masks.make_identity(nc, identity[:])

@@ -11,9 +11,10 @@ P = 128
 SCALING = 2.0
 FLOPS = 2 * N * (D * M + D * M + M * OD)
 
-LOAD_STARTS = (0, 2, 4, 8, 12, 16)
 GROUP = 2
 GROUPS = V // P // GROUP
+LOAD = 2
+LOADS = GROUPS // LOAD
 PIECES = 2
 PIECE = N // PIECES
 BLOCKS = PIECE // P
@@ -28,21 +29,21 @@ def tile_moelora_kernel(tc, table, a, w_route, bw, offs, out):
         tc.psum_pool(name="single", bufs=1) as single,
         tc.psum_pool(name="work", bufs=6) as work,
     ):
-        table_sb = held.tile([P, V // P, D], BF16, name="table_sb")
-        table_blocks = table.rearrange("(b p) d -> p b d", p=P)
+        table_sb = held.tile([P, GROUPS, GROUP, D], BF16, name="table_sb")
+        table_groups = table.rearrange("(g p k) d -> p g k d", p=P, k=GROUP)
         w_sb = held.tile([D, M], BF16, name="w_sb")
         offsets = held.tile([P, N // 16], U16, name="offsets")
         a_sb = held.tile([D, M], BF16, name="a_sb")
         bw_sb = held.tile([M, OD], BF16, name="bw_sb")
 
         nc.scalar.dma_start(w_sb[:], w_route)
-        for q in range(len(LOAD_STARTS) - 1):
-            queue = nc.scalar if q in (2, 4) else nc.sync
-            blocks = slice(LOAD_STARTS[q], LOAD_STARTS[q + 1])
-            queue.dma_start(table_sb[:, blocks, :], table_blocks[:, blocks, :])
+        for q in range(LOADS):
+            queue = nc.sync if q < LOADS - 1 else nc.scalar
+            groups = slice(q * LOAD, (q + 1) * LOAD)
+            queue.dma_start(table_sb[:, groups, :, :], table_groups[:, groups, :, :])
         nc.sync.dma_start(offsets[:], offs)
         nc.scalar.dma_start(a_sb[:], a)
-        nc.sync.dma_start(bw_sb[:], bw)
+        nc.scalar.dma_start(bw_sb[:], bw)
 
         identity = held.tile([P, P], BF16, name="identity")
         masks.make_identity(nc, identity[:])
@@ -67,12 +68,13 @@ def tile_moelora_kernel(tc, table, a, w_route, bw, offs, out):
         for g in range(GROUPS):
             turned_ps = work.tile([D, GROUP * P], BF16, name="turned_ps", tag="work")
             for k in range(GROUP):
-                nc.tensor.transpose(turned_ps[:, k * P : (k + 1) * P], table_sb[:, g * GROUP + k, :], identity[:])
-            columns = slice(g * GROUP * P, (g + 1) * GROUP * P)
+                nc.tensor.transpose(turned_ps[:, k * P : (k + 1) * P], table_sb[:, g, k, :], identity[:])
+            in_token_order = turned_ps[:].rearrange("d (k p) -> d p k", k=GROUP)
+            columns = table_t[:, g * GROUP * P : (g + 1) * GROUP * P].rearrange("d (p k) -> d p k", k=GROUP)
             if g % 2 == 0:
-                nc.scalar.copy(table_t[:, columns], turned_ps[:])
+                nc.scalar.copy(columns, in_token_order)
             else:
-                nc.vector.tensor_copy(table_t[:, columns], turned_ps[:])
+                nc.vector.tensor_copy(columns, in_token_order)
 
         list_piece = [offsets[:, i * (PIECE // 16) : (i + 1) * (PIECE // 16)] for i in range(PIECES)]
         tokens = [slice(i * PIECE, (i + 1) * PIECE) for i in range(PIECES)]

import concourse.masks as masks
import concourse.mybir as mybir

BF16, F32, U16 = mybir.dt.bfloat16, mybir.dt.float32, mybir.dt.uint16
ACT = mybir.ActivationFunctionType
ALU = mybir.AluOpType

V, D, E, R, OD, N = 2048, 128, 8, 16, 256, 512
M = E * R
P = 128
SCALING = 2.0
FLOPS = 2 * N * (D * M + D * M + M * OD)

GROUP = 2
GROUPS = V // P // GROUP
LOAD = 2
LOADS = GROUPS // LOAD
PIECES = 2
PIECE = N // PIECES
BLOCKS = PIECE // P

EXP_CAP = 1.0e30


def tile_moelora_kernel(tc, table, a, w_route, bw, offs, out):
    nc = tc.nc
    with (
        tc.tile_pool(name="held", bufs=1) as held,
        tc.psum_pool(name="single", bufs=1) as single,
        tc.psum_pool(name="work", bufs=6) as work,
    ):
        table_sb = held.tile([P, GROUPS, GROUP, D], BF16, name="table_sb")
        table_groups = table.rearrange("(g p k) d -> p g k d", p=P, k=GROUP)
        w_sb = held.tile([D, M], BF16, name="w_sb")
        offsets = held.tile([P, N // 16], U16, name="offsets")
        a_sb = held.tile([D, M], BF16, name="a_sb")
        bw_sb = held.tile([M, OD], BF16, name="bw_sb")

        nc.scalar.dma_start(w_sb[:], w_route)
        for q in range(LOADS):
            queue = nc.sync if q < LOADS - 1 else nc.scalar
            groups = slice(q * LOAD, (q + 1) * LOAD)
            queue.dma_start(table_sb[:, groups, :, :], table_groups[:, groups, :, :])
        nc.sync.dma_start(offsets[:], offs)
        nc.scalar.dma_start(a_sb[:], a)
        nc.scalar.dma_start(bw_sb[:], bw)

        identity = held.tile([P, P], BF16, name="identity")
        masks.make_identity(nc, identity[:])
        identity_f32 = held.tile([P, P], F32, name="identity_f32")
        nc.vector.tensor_copy(identity_f32[:], identity[:])

        in_expert = held.tile([M, E], F32, name="in_expert")
        nc.vector.reduce_sum(in_expert[:], identity[:].rearrange("k (e r) -> k e r", r=R), axis=mybir.AxisListType.X)
        adder = held.tile([M, E], BF16, name="adder")
        nc.vector.tensor_scalar_mul(adder[:], in_expert[:], 1.0 / (2.0 * SCALING))

        w_diff = held.tile([D, M], BF16, name="w_diff")
        w_of_f = w_sb[:].rearrange("d (f r) -> d f r", r=R)[:, :, 0]
        nc.vector.tensor_tensor(
            w_diff[:].rearrange("d (c f) -> d c f", f=E),
            w_of_f.unsqueeze(1).to_broadcast([D, M // E, E]),
            w_sb[:].rearrange("d (c f) -> d c f", f=E),
            ALU.subtract,
        )

        table_t = held.tile([D, V], BF16, name="table_t")
        for g in range(GROUPS):
            turned_ps = work.tile([D, GROUP * P], BF16, name="turned_ps", tag="work")
            for k in range(GROUP):
                nc.tensor.transpose(turned_ps[:, k * P : (k + 1) * P], table_sb[:, g, k, :], identity[:])
            in_token_order = turned_ps[:].rearrange("d (k p) -> d p k", k=GROUP)
            columns = table_t[:, g * GROUP * P : (g + 1) * GROUP * P].rearrange("d (p k) -> d p k", k=GROUP)
            if g % 2 == 0:
                nc.scalar.copy(columns, in_token_order)
            else:
                nc.vector.tensor_copy(columns, in_token_order)

        list_piece = [offsets[:, i * (PIECE // 16) : (i + 1) * (PIECE // 16)] for i in range(PIECES)]
        tokens = [slice(i * PIECE, (i + 1) * PIECE) for i in range(PIECES)]

        diff_ps = [work.tile([M, PIECE], F32, name=f"diff_ps{i}", tag="work") for i in range(PIECES)]
        for i in range(PIECES):
            nc.tensor.matmul(diff_ps[i][:], w_diff[:], table_t[:].indirect(list_piece[i]), start=True, stop=True)
        h_ps = single.tile([M, N], F32, name="h_ps")
        for i in range(PIECES):
            nc.tensor.matmul(h_ps[:, tokens[i]], a_sb[:], table_t[:].indirect(list_piece[i]), start=True, stop=True)

        expd = held.tile([M, N], BF16, name="expd")
        for i in range(PIECES):
            nc.scalar.activation(expd[:, tokens[i]], diff_ps[i][:], ACT.Exp)
            nc.vector.tensor_scalar_min(expd[:, tokens[i]], expd[:, tokens[i]], EXP_CAP)

        h_sb = held.tile([M, N], F32, name="h_sb")
        nc.scalar.copy(h_sb[:], h_ps[:])

        denom_t_ps = single.tile([P, (N // P) * E], F32, name="denom_t_ps")
        route_t = held.tile([P, (N // P) * E], F32, name="route_t")
        route_t_rows = held.tile([P, N], F32, name="route_t_rows")
        for i in range(PIECES):
            for b in range(i * BLOCKS, (i + 1) * BLOCKS):
                nc.tensor.matmul(
                    denom_t_ps[:, b * E : (b + 1) * E], expd[:, b * P : (b + 1) * P], adder[:], start=True, stop=True
                )
            experts = slice(i * BLOCKS * E, (i + 1) * BLOCKS * E)
            nc.vector.reciprocal(route_t[:, experts], denom_t_ps[:, experts])
            nc.vector.tensor_copy(
                route_t_rows[:, tokens[i]].rearrange("t (c r) -> t c r", r=R),
                route_t[:, experts].unsqueeze(2).to_broadcast([P, BLOCKS * E, R]),
            )

        wh = held.tile([M, N], BF16, name="wh")
        for i in range(PIECES):
            route_ps = work.tile([M, PIECE], F32, name="route_ps", tag="work")
            for k in range(BLOCKS):
                b = i * BLOCKS + k
                nc.tensor.transpose(route_ps[:, k * P : (k + 1) * P], route_t_rows[:, b * P : (b + 1) * P], identity_f32[:])
            nc.vector.tensor_tensor(wh[:, tokens[i]], route_ps[:], h_sb[:, tokens[i]], ALU.mult)

        for i in range(PIECES):
            for ob in range(OD // P):
                features = slice(ob * P, (ob + 1) * P)
                out_ps = work.tile([P, PIECE], F32, name="out_ps", tag="work")
                nc.tensor.matmul(out_ps[:], bw_sb[:, features], wh[:, tokens[i]], start=True, stop=True)
                out_sb = held.tile([P, PIECE], F32, name=f"out_sb{i}{ob}")
                if ob == 0:
                    nc.vector.tensor_copy(out_sb[:], out_ps[:])
                    nc.sync.dma_start(out[features, tokens[i]], out_sb[:])
                else:
                    nc.scalar.copy(out_sb[:], out_ps[:])
                    nc.scalar.dma_start(out[features, tokens[i]], out_sb[:])
